import numpy as np
import ml_dtypes


def mxq(x, axis, fmt="e4m3"):
    dtype, down = {"e4m3": (ml_dtypes.float8_e4m3fn, 7), "e5m2": (ml_dtypes.float8_e5m2, 14)}[fmt]
    v = np.moveaxis(np.asarray(x, np.float32).astype(ml_dtypes.bfloat16).astype(np.float64), axis, -1)
    blocks = v.reshape(v.shape[:-1] + (-1, 32))
    amax = np.abs(blocks).max(-1, keepdims=True)
    byte = np.maximum(np.where(amax > 0, np.frexp(amax)[1] - 1 + 127, 0) - down, 1)
    scale = np.exp2(byte - 127.0)
    codes = (blocks / scale).astype(np.float32).astype(dtype).astype(np.float64)
    return np.moveaxis((codes * scale).reshape(v.shape), -1, axis)


WIDE = False


def mx_kscale(k):
    if not WIDE:
        return np.ones(k)
    levels = np.array([10, -10, 5, -5, 0])
    a = np.random.permutation(np.resize(levels, k // 512 * 4)).reshape(k // 512, 4)
    idx = np.arange(k)
    return np.exp2(a[idx // 512, idx % 128 // 32])


BF16 = ml_dtypes.bfloat16


def bf(x):
    return np.asarray(x, np.float32).astype(BF16)


def f64(x):
    return np.asarray(x).astype(np.float64)


B, CIN, COUT, H, W = 4, 512, 512, 32, 32


def setup_inputs():
    s = mx_kscale(CIN)
    x = np.random.standard_normal((B, CIN, H, W)) * s[None, :, None, None]
    weight = np.random.uniform(-1.0, 1.0, (CIN, COUT)) * np.sqrt(3.0 / CIN) / s[:, None]
    return {"x": bf(x), "weight": bf(weight)}


def reference(x, weight):
    wq = mxq(f64(weight), 0, "e4m3")
    xq = mxq(f64(x), 1, "e4m3")
    return np.einsum("io,bihw->bohw", wq, xq, optimize=True)

@@ -1,0 +1,129 @@
+from contextlib import ExitStack
+
+import concourse.mybir as mybir
+
+BF16 = mybir.dt.bfloat16
+F32 = mybir.dt.float32
+U32 = mybir.dt.uint32
+U8 = mybir.dt.uint8
+FP8X4 = mybir.dt.float8_e4m3fn_x4
+
+P = 128
+PACK = 4
+B, CIN, COUT, PIX = 4, 512, 512, 1024
+N_TILE = 512
+HALVES = PIX // N_TILE
+M_TILES = COUT // P
+UNITS = B * HALVES
+RUN = 4
+
+FLOPS = 2 * CIN * COUT * B * PIX
+
+VECTOR_BANKS = ((7,), (7,), (7,), (1, 3, 5, 7))
+SCALAR_REGROUPS = (1,)
+
+
+def tile_simpleconvolution_kernel(tc, x, weight, out):
+    nc = tc.nc
+    with ExitStack() as ctx:
+        keep = ctx.enter_context(tc.tile_pool(name="keep", bufs=1))
+        psum = ctx.enter_context(tc.psum_pool(name="psum", bufs=1))
+        ctx.enter_context(tc.manual_schedule())
+
+        w_raw = keep.tile([P, PACK, COUT], BF16, name="w_raw")
+        nc.sync.dma_start(out=w_raw[:], in_=weight.rearrange("(p j) o -> p j o", j=PACK))
+        x_raw = []
+        for b in range(B):
+            raw = keep.tile([P, PACK, PIX], BF16, name="x_raw%d" % b)
+            nc.sync.dma_start(out=raw[:], in_=x[b].rearrange("(p j) h w -> p j (h w)", j=PACK))
+            x_raw.append(raw)
+
+        w_grouped = keep.tile([P, M_TILES, P, PACK], BF16, name="w_grouped", align_bytes=64)
+        w_codes = keep.tile([P, COUT], U32, name="w_codes", align_bytes=64)
+        w_scales = keep.tile([P, COUT], U8, name="w_scales", align_bytes=64)
+        nc.vector.tensor_copy(
+            out=w_grouped[:], in_=w_raw[:].rearrange("p j (q m) -> p m q j", m=M_TILES)
+        )
+        nc.vector.quantize_mx(
+            out=w_codes[:].bitcast(FP8X4),
+            scales=w_scales[:],
+            in_=w_grouped[:].rearrange("p m q j -> p (m q j)"),
+        )
+
+        x_grouped = []
+        x_codes = []
+        x_scales = []
+        for u in range(UNITS):
+            x_grouped.append(keep.tile([P, N_TILE, PACK], BF16, name="x_grouped%d" % u, align_bytes=64))
+            x_codes.append(keep.tile([P, N_TILE], U32, name="x_codes%d" % u, align_bytes=64))
+            x_scales.append(keep.tile([P, N_TILE], U8, name="x_scales%d" % u, align_bytes=64))
+
+        def regroup(u):
+            b, h = divmod(u, HALVES)
+            src = x_raw[b][:, :, h * N_TILE : (h + 1) * N_TILE].rearrange("p t (c i) -> p c t i", i=RUN)
+            dst = x_grouped[u][:].rearrange("p (c i) t -> p c t i", i=RUN)
+            if u in SCALAR_REGROUPS:
+                nc.scalar.copy(out=dst, in_=src)
+            else:
+                nc.vector.tensor_copy(out=dst, in_=src)
+
+        def quantise(u):
+            nc.vector.quantize_mx(
+                out=x_codes[u][:].bitcast(FP8X4),
+                scales=x_scales[u][:],
+                in_=x_grouped[u][:].rearrange("p w t -> p (w t)"),
+            )
+
+        out_views = [out[b].rearrange("(p m) h w -> p m (h w)", m=M_TILES) for b in range(B)]
+        results = {}
+        banks = {}
+
+        def multiply(b, k):
+            pair, rest = divmod(k, 4)
+            h, mi = divmod(rest, 2)
+            m = 2 * pair + mi
+            acc = psum.tile([P, N_TILE], F32, name="acc%d" % k)
+            nc.tensor.matmul_mx(
+                out=acc[:],
+                lhsT=w_codes[:, m * P : (m + 1) * P].bitcast(FP8X4),
+                lhsT_scale=w_scales[:, m * P : (m + 1) * P],
+                rhs=x_codes[b * HALVES + h][:].bitcast(FP8X4),
+                rhs_scale=x_scales[b * HALVES + h][:],
+                start=True,
+                stop=True,
+            )
+            banks[(b, k)] = acc
+
+        def empty(b, k):
+            pair, rest = divmod(k, 4)
+            h, mi = divmod(rest, 2)
+            dst = results[(b, pair)][:, mi, h * N_TILE : (h + 1) * N_TILE]
+            if k in VECTOR_BANKS[b]:
+                nc.vector.tensor_copy(out=dst, in_=banks[(b, k)][:])
+            else:
+                nc.scalar.copy(out=dst, in_=banks[(b, k)][:])
+
+        def store(b, pair):
+            nc.sync.dma_start(
+                out=out_views[b][:, 2 * pair : 2 * pair + 2, :], in_=results[(b, pair)][:]
+            )
+
+        for b in range(B):
+            for pair in range(2):
+                results[(b, pair)] = keep.tile([P, 2, PIX], F32, name="result%d_%d" % (b, pair))
+            regroup(2 * b)
+            regroup(2 * b + 1)
+            quantise(2 * b)
+            quantise(2 * b + 1)
+            if b > 0:
+                empty(b - 1, 7)
+                store(b - 1, 1)
+            last = b == B - 1
+            for k in range(8):
+                multiply(b, k)
+                if k < 7 or last:
+                    empty(b, k)
+                if k == 3:
+                    store(b, 0)
+            if last:
+                store(b, 1)

@@ -19,6 +19,7 @@ RUN = 4
 
 FLOPS = 2 * CIN * COUT * B * PIX
 
+STORE_GROUPS = (((0,), (1,), (2, 3)), ((0, 1), (2, 3)), ((0, 1), (2, 3)), ((0, 1), (2, 3)))
 VECTOR_BANKS = ((7,), (7,), (7,), (1, 3, 5, 7))
 SCALAR_REGROUPS = (1,)
 
@@ -75,13 +76,9 @@ def tile_simpleconvolution_kernel(tc, x, weight, out):
             )
 
         out_views = [out[b].rearrange("(p m) h w -> p m (h w)", m=M_TILES) for b in range(B)]
-        results = {}
         banks = {}
 
-        def multiply(b, k):
-            pair, rest = divmod(k, 4)
-            h, mi = divmod(rest, 2)
-            m = 2 * pair + mi
+        def multiply(b, k, m, h):
             acc = psum.tile([P, N_TILE], F32, name="acc%d" % k)
             nc.tensor.matmul_mx(
                 out=acc[:],
@@ -94,36 +91,39 @@ def tile_simpleconvolution_kernel(tc, x, weight, out):
             )
             banks[(b, k)] = acc
 
-        def empty(b, k):
-            pair, rest = divmod(k, 4)
-            h, mi = divmod(rest, 2)
-            dst = results[(b, pair)][:, mi, h * N_TILE : (h + 1) * N_TILE]
+        def empty(b, k, dst):
             if k in VECTOR_BANKS[b]:
                 nc.vector.tensor_copy(out=dst, in_=banks[(b, k)][:])
             else:
                 nc.scalar.copy(out=dst, in_=banks[(b, k)][:])
 
-        def store(b, pair):
-            nc.sync.dma_start(
-                out=out_views[b][:, 2 * pair : 2 * pair + 2, :], in_=results[(b, pair)][:]
-            )
+        def store(b, group, result):
+            nc.sync.dma_start(out=out_views[b][:, group[0] : group[-1] + 1, :], in_=result[:])
 
+        held = []
         for b in range(B):
-            for pair in range(2):
-                results[(b, pair)] = keep.tile([P, 2, PIX], F32, name="result%d_%d" % (b, pair))
             regroup(2 * b)
             regroup(2 * b + 1)
             quantise(2 * b)
+            for late in held:
+                empty(late[0], late[1], late[2])
+                store(late[0], late[3], late[4])
+            held = []
             quantise(2 * b + 1)
-            if b > 0:
-                empty(b - 1, 7)
-                store(b - 1, 1)
             last = b == B - 1
-            for k in range(8):
-                multiply(b, k)
-                if k < 7 or last:
-                    empty(b, k)
-                if k == 3:
-                    store(b, 0)
-            if last:
-                store(b, 1)
+            k = 0
+            for group in STORE_GROUPS[b]:
+                result = keep.tile([P, len(group), PIX], F32, name="result%d_%d" % (b, group[0]))
+                waits = False
+                for h in range(HALVES):
+                    for mi in range(len(group)):
+                        dst = result[:, mi, h * N_TILE : (h + 1) * N_TILE]
+                        multiply(b, k, group[mi], h)
+                        if k == 7 and not last:
+                            held.append((b, k, dst, group, result))
+                            waits = True
+                        else:
+                            empty(b, k, dst)
+                        k += 1
+                if not waits:
+                    store(b, group, result)

@@ -43,7 +43,7 @@ def tile_simpleconvolution_kernel(tc, x, weight, out):
         w_codes = keep.tile([P, COUT], U32, name="w_codes", align_bytes=64)
         w_scales = keep.tile([P, COUT], U8, name="w_scales", align_bytes=64)
         nc.vector.tensor_copy(
-            out=w_grouped[:], in_=w_raw[:].rearrange("p j (q m) -> p m q j", m=M_TILES)
+            out=w_grouped[:], in_=w_raw[:].rearrange("p j (m q) -> p m q j", m=M_TILES)
         )
         nc.vector.quantize_mx(
             out=w_codes[:].bitcast(FP8X4),
@@ -75,7 +75,7 @@ def tile_simpleconvolution_kernel(tc, x, weight, out):
                 in_=x_grouped[u][:].rearrange("p w t -> p (w t)"),
             )
 
-        out_views = [out[b].rearrange("(p m) h w -> p m (h w)", m=M_TILES) for b in range(B)]
+        out_views = [out[b].rearrange("(m p) h w -> p m (h w)", m=M_TILES) for b in range(B)]
         banks = {}
 
         def multiply(b, k, m, h):

@@ -19,7 +19,7 @@ RUN = 4
 
 FLOPS = 2 * CIN * COUT * B * PIX
 
-STORE_GROUPS = (((0,), (1,), (2, 3)), ((0, 1), (2, 3)), ((0, 1), (2, 3)), ((0, 1), (2, 3)))
+STORE_GROUPS = (((0,), (1,), (2, 3)), ((0, 1), (2, 3)), ((0, 1), (2, 3)), ((0, 1, 2, 3),))
 VECTOR_BANKS = ((7,), (7,), (7,), (1, 3, 5, 7))
 SCALAR_REGROUPS = (1,)
 
@@ -43,7 +43,7 @@ def tile_simpleconvolution_kernel(tc, x, weight, out):
         w_codes = keep.tile([P, COUT], U32, name="w_codes", align_bytes=64)
         w_scales = keep.tile([P, COUT], U8, name="w_scales", align_bytes=64)
         nc.vector.tensor_copy(
-            out=w_grouped[:], in_=w_raw[:].rearrange("p j (m q) -> p m q j", m=M_TILES)
+            out=w_grouped[:], in_=w_raw[:].rearrange("p j (q m) -> p m q j", m=M_TILES)
         )
         nc.vector.quantize_mx(
             out=w_codes[:].bitcast(FP8X4),
@@ -75,7 +75,7 @@ def tile_simpleconvolution_kernel(tc, x, weight, out):
                 in_=x_grouped[u][:].rearrange("p w t -> p (w t)"),
             )
 
-        out_views = [out[b].rearrange("(m p) h w -> p m (h w)", m=M_TILES) for b in range(B)]
+        out_views = [out[b].rearrange("(p m) h w -> p m (h w)", m=M_TILES) for b in range(B)]
         banks = {}
 
         def multiply(b, k, m, h):

@@ -21,7 +21,8 @@ FLOPS = 2 * CIN * COUT * B * PIX
 
 STORE_GROUPS = (((0,), (1,), (2, 3)), ((0, 1), (2, 3)), ((0, 1), (2, 3)), ((0, 1, 2, 3),))
 VECTOR_BANKS = ((7,), (7,), (7,), (1, 3, 5, 7))
-SCALAR_REGROUPS = (1,)
+SCALAR_COLUMNS = 320
+WARM_UP = 8
 
 
 def tile_simpleconvolution_kernel(tc, x, weight, out):
@@ -38,6 +39,10 @@ def tile_simpleconvolution_kernel(tc, x, weight, out):
             raw = keep.tile([P, PACK, PIX], BF16, name="x_raw%d" % b)
             nc.sync.dma_start(out=raw[:], in_=x[b].rearrange("(p j) h w -> p j (h w)", j=PACK))
             x_raw.append(raw)
+
+        warm = psum.tile([P, N_TILE], F32, name="acc7")
+        for i in range(WARM_UP):
+            nc.tensor.matmul(out=warm[:], lhsT=w_raw[:, 0, 0:P], rhs=w_raw[:, 1, :], start=True, stop=True)
 
         w_grouped = keep.tile([P, M_TILES, P, PACK], BF16, name="w_grouped", align_bytes=64)
         w_codes = keep.tile([P, COUT], U32, name="w_codes", align_bytes=64)
@@ -59,11 +64,11 @@ def tile_simpleconvolution_kernel(tc, x, weight, out):
             x_codes.append(keep.tile([P, N_TILE], U32, name="x_codes%d" % u, align_bytes=64))
             x_scales.append(keep.tile([P, N_TILE], U8, name="x_scales%d" % u, align_bytes=64))
 
-        def regroup(u):
+        def regroup(u, first=0, end=N_TILE, scalar=False):
             b, h = divmod(u, HALVES)
-            src = x_raw[b][:, :, h * N_TILE : (h + 1) * N_TILE].rearrange("p t (c i) -> p c t i", i=RUN)
-            dst = x_grouped[u][:].rearrange("p (c i) t -> p c t i", i=RUN)
-            if u in SCALAR_REGROUPS:
+            src = x_raw[b][:, :, h * N_TILE + first : h * N_TILE + end].rearrange("p t (c i) -> p c t i", i=RUN)
+            dst = x_grouped[u][:, first:end, :].rearrange("p (c i) t -> p c t i", i=RUN)
+            if scalar:
                 nc.scalar.copy(out=dst, in_=src)
             else:
                 nc.vector.tensor_copy(out=dst, in_=src)
@@ -103,7 +108,11 @@ def tile_simpleconvolution_kernel(tc, x, weight, out):
         held = []
         for b in range(B):
             regroup(2 * b)
-            regroup(2 * b + 1)
+            if b == 0:
+                regroup(1, 0, SCALAR_COLUMNS, scalar=True)
+                regroup(1, SCALAR_COLUMNS, N_TILE)
+            else:
+                regroup(2 * b + 1)
             quantise(2 * b)
             for late in held:
                 empty(late[0], late[1], late[2])

@@ -20,8 +20,8 @@ RUN = 4
 FLOPS = 2 * CIN * COUT * B * PIX
 
 STORE_GROUPS = (((0,), (1,), (2, 3)), ((0, 1), (2, 3)), ((0, 1), (2, 3)), ((0, 1, 2, 3),))
-VECTOR_BANKS = ((7,), (7,), (7,), (1, 3, 5, 7))
-SCALAR_COLUMNS = 320
+VECTOR_BANKS = ((7,), (7,), (), (1, 3, 5, 7))
+SCALAR_COLUMNS = 432
 WARM_UP = 8
 
 
@@ -128,7 +128,7 @@ def tile_simpleconvolution_kernel(tc, x, weight, out):
                     for mi in range(len(group)):
                         dst = result[:, mi, h * N_TILE : (h + 1) * N_TILE]
                         multiply(b, k, group[mi], h)
-                        if k == 7 and not last:
+                        if k in VECTOR_BANKS[b] and not last:
                             held.append((b, k, dst, group, result))
                             waits = True
                         else:

@@ -19,7 +19,7 @@ RUN = 4
 
 FLOPS = 2 * CIN * COUT * B * PIX
 
-STORE_GROUPS = (((0,), (1,), (2, 3)), ((0, 1), (2, 3)), ((0, 1), (2, 3)), ((0, 1, 2, 3),))
+STORE_GROUPS = (((0,), (1,), (2,), (3,)), ((0, 1), (2, 3)), ((0, 1), (2, 3)), ((0, 1, 2, 3),))
 VECTOR_BANKS = ((7,), (7,), (), (1, 3, 5, 7))
 SCALAR_COLUMNS = 432
 WARM_UP = 8

@@ -19,8 +19,9 @@ RUN = 4
 
 FLOPS = 2 * CIN * COUT * B * PIX
 
-STORE_GROUPS = (((0,), (1,), (2,), (3,)), ((0, 1), (2, 3)), ((0, 1), (2, 3)), ((0, 1, 2, 3),))
-VECTOR_BANKS = ((7,), (7,), (), (1, 3, 5, 7))
+BANK_RUNS = (((0,), (1,), (2,), (3,)), ((0, 1), (2, 3)), ((0, 1), (2, 3)), ((0, 1, 2, 3),))
+STORE_GROUPS = (((0,), (1,), (2,), (3,)), ((0,), (1,), (2, 3)), ((0, 1), (2, 3)), ((0, 1, 2, 3),))
+VECTOR_BANKS = ((7,), (7,), (7,), (1, 3, 5, 7))
 SCALAR_COLUMNS = 432
 WARM_UP = 8
 
@@ -96,14 +97,19 @@ def tile_simpleconvolution_kernel(tc, x, weight, out):
             )
             banks[(b, k)] = acc
 
-        def empty(b, k, dst):
+        place = {}
+        full = {}
+
+        def empty(b, k, m, h):
+            result, mi, group = place[(b, m)]
+            dst = result[:, mi, h * N_TILE : (h + 1) * N_TILE]
             if k in VECTOR_BANKS[b]:
                 nc.vector.tensor_copy(out=dst, in_=banks[(b, k)][:])
             else:
                 nc.scalar.copy(out=dst, in_=banks[(b, k)][:])
-
-        def store(b, group, result):
-            nc.sync.dma_start(out=out_views[b][:, group[0] : group[-1] + 1, :], in_=result[:])
+            full[(b, group)] -= 1
+            if full[(b, group)] == 0:
+                nc.sync.dma_start(out=out_views[b][:, group[0] : group[-1] + 1, :], in_=result[:])
 
         held = []
         for b in range(B):
@@ -115,24 +121,22 @@ def tile_simpleconvolution_kernel(tc, x, weight, out):
                 regroup(2 * b + 1)
             quantise(2 * b)
             for late in held:
-                empty(late[0], late[1], late[2])
-                store(late[0], late[3], late[4])
+                empty(late[0], late[1], late[2], late[3])
             held = []
             quantise(2 * b + 1)
             last = b == B - 1
-            k = 0
             for group in STORE_GROUPS[b]:
                 result = keep.tile([P, len(group), PIX], F32, name="result%d_%d" % (b, group[0]))
-                waits = False
+                full[(b, group)] = HALVES * len(group)
+                for mi in range(len(group)):
+                    place[(b, group[mi])] = (result, mi, group)
+            k = 0
+            for run in BANK_RUNS[b]:
                 for h in range(HALVES):
-                    for mi in range(len(group)):
-                        dst = result[:, mi, h * N_TILE : (h + 1) * N_TILE]
-                        multiply(b, k, group[mi], h)
+                    for m in run:
+                        multiply(b, k, m, h)
                         if k in VECTOR_BANKS[b] and not last:
-                            held.append((b, k, dst, group, result))
-                            waits = True
+                            held.append((b, k, m, h))
                         else:
-                            empty(b, k, dst)
+                            empty(b, k, m, h)
                         k += 1
-                if not waits:
-                    store(b, group, result)

@@ -23,7 +23,8 @@ BANK_RUNS = (((0,), (1,), (2,), (3,)), ((0, 1), (2, 3)), ((0, 1), (2, 3)), ((0, 
 STORE_GROUPS = (((0,), (1,), (2,), (3,)), ((0,), (1,), (2, 3)), ((0, 1), (2, 3)), ((0, 1, 2, 3),))
 VECTOR_BANKS = ((7,), (7,), (7,), (1, 3, 5, 7))
 SCALAR_COLUMNS = 432
-WARM_UP = 8
+WARM_UP_WEIGHT = 6
+WARM_UP_BATCH = 5
 
 
 def tile_simpleconvolution_kernel(tc, x, weight, out):
@@ -42,8 +43,10 @@ def tile_simpleconvolution_kernel(tc, x, weight, out):
             x_raw.append(raw)
 
         warm = psum.tile([P, N_TILE], F32, name="acc7")
-        for i in range(WARM_UP):
+        for i in range(WARM_UP_WEIGHT):
             nc.tensor.matmul(out=warm[:], lhsT=w_raw[:, 0, 0:P], rhs=w_raw[:, 1, :], start=True, stop=True)
+        for i in range(WARM_UP_BATCH):
+            nc.tensor.matmul(out=warm[:], lhsT=x_raw[0][:, 0, 0:P], rhs=x_raw[0][:, 1, 0:N_TILE], start=True, stop=True)
 
         w_grouped = keep.tile([P, M_TILES, P, PACK], BF16, name="w_grouped", align_bytes=64)
         w_codes = keep.tile([P, COUT], U32, name="w_codes", align_bytes=64)

from contextlib import ExitStack

import concourse.mybir as mybir

BF16 = mybir.dt.bfloat16
F32 = mybir.dt.float32
U32 = mybir.dt.uint32
U8 = mybir.dt.uint8
FP8X4 = mybir.dt.float8_e4m3fn_x4

P = 128
PACK = 4
B, CIN, COUT, PIX = 4, 512, 512, 1024
N_TILE = 512
HALVES = PIX // N_TILE
M_TILES = COUT // P
UNITS = B * HALVES
RUN = 4

FLOPS = 2 * CIN * COUT * B * PIX

BANK_RUNS = (((0,), (1,), (2,), (3,)), ((0, 1), (2, 3)), ((0, 1), (2, 3)), ((0, 1, 2, 3),))
STORE_GROUPS = (((0,), (1,), (2,), (3,)), ((0,), (1,), (2, 3)), ((0, 1), (2, 3)), ((0, 1, 2, 3),))
VECTOR_BANKS = ((7,), (7,), (7,), (1, 3, 5, 7))
SCALAR_COLUMNS = 432
WARM_UP_WEIGHT = 6
WARM_UP_BATCH = 5


def tile_simpleconvolution_kernel(tc, x, weight, out):
    nc = tc.nc
    with ExitStack() as ctx:
        keep = ctx.enter_context(tc.tile_pool(name="keep", bufs=1))
        psum = ctx.enter_context(tc.psum_pool(name="psum", bufs=1))
        ctx.enter_context(tc.manual_schedule())

        w_raw = keep.tile([P, PACK, COUT], BF16, name="w_raw")
        nc.sync.dma_start(out=w_raw[:], in_=weight.rearrange("(p j) o -> p j o", j=PACK))
        x_raw = []
        for b in range(B):
            raw = keep.tile([P, PACK, PIX], BF16, name="x_raw%d" % b)
            nc.sync.dma_start(out=raw[:], in_=x[b].rearrange("(p j) h w -> p j (h w)", j=PACK))
            x_raw.append(raw)

        warm = psum.tile([P, N_TILE], F32, name="acc7")
        for i in range(WARM_UP_WEIGHT):
            nc.tensor.matmul(out=warm[:], lhsT=w_raw[:, 0, 0:P], rhs=w_raw[:, 1, :], start=True, stop=True)
        for i in range(WARM_UP_BATCH):
            nc.tensor.matmul(out=warm[:], lhsT=x_raw[0][:, 0, 0:P], rhs=x_raw[0][:, 1, 0:N_TILE], start=True, stop=True)

        w_grouped = keep.tile([P, M_TILES, P, PACK], BF16, name="w_grouped", align_bytes=64)
        w_codes = keep.tile([P, COUT], U32, name="w_codes", align_bytes=64)
        w_scales = keep.tile([P, COUT], U8, name="w_scales", align_bytes=64)
        nc.vector.tensor_copy(
            out=w_grouped[:], in_=w_raw[:].rearrange("p j (q m) -> p m q j", m=M_TILES)
        )
        nc.vector.quantize_mx(
            out=w_codes[:].bitcast(FP8X4),
            scales=w_scales[:],
            in_=w_grouped[:].rearrange("p m q j -> p (m q j)"),
        )

        x_grouped = []
        x_codes = []
        x_scales = []
        for u in range(UNITS):
            x_grouped.append(keep.tile([P, N_TILE, PACK], BF16, name="x_grouped%d" % u, align_bytes=64))
            x_codes.append(keep.tile([P, N_TILE], U32, name="x_codes%d" % u, align_bytes=64))
            x_scales.append(keep.tile([P, N_TILE], U8, name="x_scales%d" % u, align_bytes=64))

        def regroup(u, first=0, end=N_TILE, scalar=False):
            b, h = divmod(u, HALVES)
            src = x_raw[b][:, :, h * N_TILE + first : h * N_TILE + end].rearrange("p t (c i) -> p c t i", i=RUN)
            dst = x_grouped[u][:, first:end, :].rearrange("p (c i) t -> p c t i", i=RUN)
            if scalar:
                nc.scalar.copy(out=dst, in_=src)
            else:
                nc.vector.tensor_copy(out=dst, in_=src)

        def quantise(u):
            nc.vector.quantize_mx(
                out=x_codes[u][:].bitcast(FP8X4),
                scales=x_scales[u][:],
                in_=x_grouped[u][:].rearrange("p w t -> p (w t)"),
            )

        out_views = [out[b].rearrange("(p m) h w -> p m (h w)", m=M_TILES) for b in range(B)]
        banks = {}

        def multiply(b, k, m, h):
            acc = psum.tile([P, N_TILE], F32, name="acc%d" % k)
            nc.tensor.matmul_mx(
                out=acc[:],
                lhsT=w_codes[:, m * P : (m + 1) * P].bitcast(FP8X4),
                lhsT_scale=w_scales[:, m * P : (m + 1) * P],
                rhs=x_codes[b * HALVES + h][:].bitcast(FP8X4),
                rhs_scale=x_scales[b * HALVES + h][:],
                start=True,
                stop=True,
            )
            banks[(b, k)] = acc

        place = {}
        full = {}

        def empty(b, k, m, h):
            result, mi, group = place[(b, m)]
            dst = result[:, mi, h * N_TILE : (h + 1) * N_TILE]
            if k in VECTOR_BANKS[b]:
                nc.vector.tensor_copy(out=dst, in_=banks[(b, k)][:])
            else:
                nc.scalar.copy(out=dst, in_=banks[(b, k)][:])
            full[(b, group)] -= 1
            if full[(b, group)] == 0:
                nc.sync.dma_start(out=out_views[b][:, group[0] : group[-1] + 1, :], in_=result[:])

        held = []
        for b in range(B):
            regroup(2 * b)
            if b == 0:
                regroup(1, 0, SCALAR_COLUMNS, scalar=True)
                regroup(1, SCALAR_COLUMNS, N_TILE)
            else:
                regroup(2 * b + 1)
            quantise(2 * b)
            for late in held:
                empty(late[0], late[1], late[2], late[3])
            held = []
            quantise(2 * b + 1)
            last = b == B - 1
            for group in STORE_GROUPS[b]:
                result = keep.tile([P, len(group), PIX], F32, name="result%d_%d" % (b, group[0]))
                full[(b, group)] = HALVES * len(group)
                for mi in range(len(group)):
                    place[(b, group[mi])] = (result, mi, group)
            k = 0
            for run in BANK_RUNS[b]:
                for h in range(HALVES):
                    for m in run:
                        multiply(b, k, m, h)
                        if k in VECTOR_BANKS[b] and not last:
                            held.append((b, k, m, h))
                        else:
                            empty(b, k, m, h)
                        k += 1
